import numpy as np
import ml_dtypes


def mxq(x, axis, fmt="e4m3"):
    dtype, down = {"e4m3": (ml_dtypes.float8_e4m3fn, 7), "e5m2": (ml_dtypes.float8_e5m2, 14)}[fmt]
    v = np.moveaxis(np.asarray(x, np.float32).astype(ml_dtypes.bfloat16).astype(np.float64), axis, -1)
    blocks = v.reshape(v.shape[:-1] + (-1, 32))
    amax = np.abs(blocks).max(-1, keepdims=True)
    byte = np.maximum(np.where(amax > 0, np.frexp(amax)[1] - 1 + 127, 0) - down, 1)
    scale = np.exp2(byte - 127.0)
    codes = (blocks / scale).astype(np.float32).astype(dtype).astype(np.float64)
    return np.moveaxis((codes * scale).reshape(v.shape), -1, axis)


WIDE = False


def mx_kscale(k):
    if not WIDE:
        return np.ones(k)
    levels = np.array([10, -10, 5, -5, 0])
    if k % 512:
        return np.exp2(np.random.permutation(np.resize(levels, k // 32))).repeat(32)
    a = np.empty((k // 512, 16))
    for p in range(k // 512):
        a[p, :8] = np.random.permutation(np.resize(levels, 8))
        for g in range(8):
            far = levels[np.abs(levels - a[p, g]) >= 10]
            a[p, g + 8] = far[np.random.randint(len(far))]
    return np.exp2(a.ravel()).repeat(32)


BF16 = ml_dtypes.bfloat16


def bf(x):
    return np.asarray(x, np.float32).astype(BF16)


def f64(x):
    return np.asarray(x).astype(np.float64)


B, G, Z1, Z2, H, PD = 4096, 4, 256, 256, 512, 128


def glin(x, W, b):
    y = mxq(x, 2, "e4m3").transpose(1, 0, 2) @ mxq(f64(W), 2, "e4m3").transpose(0, 2, 1)
    return y.transpose(1, 0, 2) + f64(b)


def setup_inputs():
    s = mx_kscale(H)
    h = np.maximum(np.random.standard_normal((B, G, H)), 0.0) + np.maximum(np.random.standard_normal((B, G, H)), 0.0)
    return {"h": bf(h * s),
            "W3": bf(np.random.standard_normal((G, H, H)) / np.sqrt(H) * s[None, :, None] / s[None, None, :]),
            "b3": bf(np.random.standard_normal((G, H)) * 0.2 * s),
            "Wo": bf(np.random.standard_normal((G, PD, H)) * 0.6 / np.sqrt(H) / s[None, None, :]),
            "bo": bf(np.random.standard_normal((G, PD)) * 0.2)}


def reference(h, W3, b3, Wo, bo):
    h = f64(h)
    h3 = np.maximum(glin(h, W3, b3), 0.0) + h
    out = glin(h3, Wo, bo)
    return out.reshape(B, G * PD)

@@ -1,0 +1,218 @@
+from contextlib import ExitStack
+
+import concourse.mybir as mybir
+from concourse.masks import make_identity
+
+F32 = mybir.dt.float32
+BF16 = mybir.dt.bfloat16
+U32 = mybir.dt.uint32
+U8 = mybir.dt.uint8
+FP8X4 = mybir.dt.float8_e4m3fn_x4
+ADD = mybir.AluOpType.add
+RELU = mybir.ActivationFunctionType.Relu
+
+B, G, H, PD = 4096, 4, 512, 128
+P = 128
+PACK = 4
+ROW_TILES = 4
+UNIT = P * ROW_TILES
+CHUNKS = B // UNIT
+RUN = 4
+
+FLOPS = 2 * B * G * (H * H + H * PD)
+
+
+def tile_linearwdecoder_pb_t_kernel(tc, h, W3, b3, Wo, bo, out):
+    nc = tc.nc
+    with ExitStack() as ctx:
+        const = ctx.enter_context(tc.tile_pool(name="const", bufs=1))
+        weights = ctx.enter_context(tc.tile_pool(name="weights", bufs=G + 1))
+        rows_pool = ctx.enter_context(tc.tile_pool(name="rows", bufs=6))
+        grouped_pool = ctx.enter_context(tc.tile_pool(name="grouped", bufs=5))
+        mx_pool = ctx.enter_context(tc.tile_pool(name="mx", bufs=3))
+        relu_pool = ctx.enter_context(tc.tile_pool(name="relu", bufs=3))
+        h3_pool = ctx.enter_context(tc.tile_pool(name="h3", bufs=2))
+        result_pool = ctx.enter_context(tc.tile_pool(name="result", bufs=3))
+        turned_pool = ctx.enter_context(tc.psum_pool(name="turned", bufs=2))
+        hidden_pool = ctx.enter_context(tc.psum_pool(name="hidden", bufs=PACK))
+        projected_pool = ctx.enter_context(tc.psum_pool(name="projected", bufs=2))
+
+        identity = const.tile([P, P], F32)
+        make_identity(nc, identity[:])
+
+        h_units = h.rearrange("(c p i) g k -> c g p i k", p=P, i=ROW_TILES)
+        out_units = out.rearrange("(c p i) (g n) -> c g p i n", p=P, i=ROW_TILES, g=G)
+        w3_units = W3.rearrange("g (p t) k -> g p t k", t=PACK)
+
+        stream = [(Wo.rearrange("g p k -> p g k"), None, None)]
+        w3_place = []
+        for g in range(G):
+            w3_place.append(len(stream))
+            stream.append((w3_units[g], g, None))
+            for c in range(CHUNKS):
+                stream.append((h_units[c, g], g, c))
+        tiles = {}
+
+        def in_stream(n):
+            return 0 <= n < len(stream)
+
+        def is_tokens(n):
+            return in_stream(n) and stream[n][2] is not None
+
+        def is_w3(n):
+            return in_stream(n) and stream[n][1] is not None and stream[n][2] is None
+
+        def load(n):
+            if not in_stream(n):
+                return
+            view = stream[n][0]
+            rows = rows_pool.tile([P, UNIT * PACK], BF16)
+            nc.sync.dma_start(out=rows[:].rearrange("p (i k) -> p i k", i=view.shape[1]), in_=view)
+            tiles["rows", n] = rows
+            if is_w3(n):
+                g = stream[n][1]
+                b3_pairs = weights.tile([P, PACK], BF16)
+                nc.scalar.dma_start(
+                    out=b3_pairs[:],
+                    in_=b3[g].rearrange("(p t) -> p t", t=PACK),
+                )
+                bo_rows = weights.tile([P, PD], BF16)
+                nc.scalar.dma_start(out=bo_rows[:], in_=bo[g].partition_broadcast(P))
+                tiles["b3_pairs", g] = b3_pairs
+                tiles["bo_rows", g] = bo_rows
+
+        def turn(n):
+            if not in_stream(n):
+                return
+            row_words = tiles["rows", n][:].bitcast(F32)
+            for pair in range(ROW_TILES // 2):
+                turned = turned_pool.tile([P, 2, 2 * P], F32)
+                for j in range(2):
+                    for u in range(2):
+                        first = (2 * pair + j) * 2 * P
+                        nc.tensor.transpose(
+                            turned[:, u, j * P : (j + 1) * P], row_words[:, first + u : first + 2 * P : 2], identity[:]
+                        )
+                tiles["turned", n, pair] = turned
+
+        def regroup(n):
+            if not in_stream(n):
+                return
+            grouped = grouped_pool.tile([P, UNIT * PACK], BF16, align_bytes=64)
+            grouped_words = grouped[:].bitcast(F32).rearrange("p (c u) -> p c u", u=2)
+            for pair in range(ROW_TILES // 2):
+                nc.scalar.copy(
+                    out=grouped_words[:, pair * 2 * P : (pair + 1) * 2 * P, :],
+                    in_=tiles["turned", n, pair][:].rearrange("p u c -> p c u"),
+                )
+            tiles["grouped", n] = grouped
+
+        def quantise(n):
+            if not in_stream(n):
+                return
+            pool = mx_pool if is_tokens(n) else weights
+            codes = pool.tile([P, UNIT], U32, align_bytes=64)
+            scales = pool.tile([P, UNIT], U8, align_bytes=64)
+            nc.vector.quantize_mx(out=codes[:].bitcast(FP8X4), scales=scales[:], in_=tiles["grouped", n][:])
+            tiles["codes", n] = codes
+            tiles["scales", n] = scales
+            if is_w3(n):
+                g = stream[n][1]
+                b3_columns = weights.tile([P, PACK], F32)
+                nc.vector.tensor_copy(out=b3_columns[:], in_=tiles["b3_pairs", g][:])
+                tiles["b3_columns", g] = b3_columns
+
+        def multiply_w3(n):
+            if not is_tokens(n):
+                return
+            w3 = w3_place[stream[n][1]]
+            for t in range(PACK):
+                hidden = hidden_pool.tile([P, UNIT], F32)
+                nc.tensor.matmul_mx(
+                    out=hidden[:],
+                    lhsT=tiles["codes", w3][:, t * P : (t + 1) * P].bitcast(FP8X4),
+                    lhsT_scale=tiles["scales", w3][:, t * P : (t + 1) * P],
+                    rhs=tiles["codes", n][:].bitcast(FP8X4),
+                    rhs_scale=tiles["scales", n][:],
+                    start=True,
+                    stop=True,
+                )
+                tiles["hidden", n, t] = hidden
+
+        def bias_relu(n):
+            if not is_tokens(n):
+                return
+            g = stream[n][1]
+            relu = relu_pool.tile([P, PACK, UNIT], F32)
+            for t in range(PACK):
+                nc.scalar.activation(
+                    out=relu[:, t, :],
+                    in_=tiles["hidden", n, t][:],
+                    func=RELU,
+                    bias=tiles["b3_columns", g][:, t : t + 1],
+                )
+            tiles["relu", n] = relu
+
+        def add_residual(n):
+            if not is_tokens(n):
+                return
+            h3 = h3_pool.tile([P, UNIT * PACK], BF16, align_bytes=64)
+            nc.vector.tensor_tensor(
+                out=h3[:].rearrange("p (c i t) -> p c t i", i=RUN, t=PACK),
+                in0=tiles["relu", n][:].rearrange("p t (c i) -> p c t i", i=RUN),
+                in1=tiles["grouped", n][:].rearrange("p (c i t) -> p c t i", i=RUN, t=PACK),
+                op=ADD,
+            )
+            tiles["h3", n] = h3
+
+        def quantise_h3(n):
+            if not is_tokens(n):
+                return
+            h3_codes = h3_pool.tile([P, UNIT], U32, align_bytes=64)
+            h3_scales = h3_pool.tile([P, UNIT], U8, align_bytes=64)
+            nc.vector.quantize_mx(out=h3_codes[:].bitcast(FP8X4), scales=h3_scales[:], in_=tiles["h3", n][:])
+            tiles["h3_codes", n] = h3_codes
+            tiles["h3_scales", n] = h3_scales
+
+        def multiply_wo(n):
+            if not is_tokens(n):
+                return
+            g = stream[n][1]
+            projected = projected_pool.tile([P, ROW_TILES, PD], F32)
+            for i in range(ROW_TILES):
+                nc.tensor.matmul_mx(
+                    out=projected[:, i, :],
+                    lhsT=tiles["h3_codes", n][:, i * P : (i + 1) * P].bitcast(FP8X4),
+                    lhsT_scale=tiles["h3_scales", n][:, i * P : (i + 1) * P],
+                    rhs=tiles["codes", 0][:, g * PD : (g + 1) * PD].bitcast(FP8X4),
+                    rhs_scale=tiles["scales", 0][:, g * PD : (g + 1) * PD],
+                    start=True,
+                    stop=True,
+                )
+            tiles["projected", n] = projected
+
+        def finish(n):
+            if not is_tokens(n):
+                return
+            g, c = stream[n][1], stream[n][2]
+            result = result_pool.tile([P, ROW_TILES, PD], F32)
+            nc.vector.tensor_tensor(
+                out=result[:],
+                in0=tiles["projected", n][:],
+                in1=tiles["bo_rows", g][:].unsqueeze(1).to_broadcast([P, ROW_TILES, PD]),
+                op=ADD,
+            )
+            nc.sync.dma_start(out=out_units[c, g], in_=result[:])
+
+        with tc.manual_schedule():
+            for step in range(len(stream) + 7):
+                load(step)
+                quantise(step - 4)
+                turn(step - 3)
+                multiply_wo(step - 7)
+                bias_relu(step - 5)
+                multiply_w3(step - 4)
+                regroup(step - 3)
+                add_residual(step - 6)
+                finish(step - 7)
+                quantise_h3(step - 6)

@@ -17,7 +17,7 @@ PACK = 4
 ROW_TILES = 4
 UNIT = P * ROW_TILES
 CHUNKS = B // UNIT
-RUN = 4
+RUN = 2
 
 FLOPS = 2 * B * G * (H * H + H * PD)
 

@@ -16,8 +16,14 @@ P = 128
 PACK = 4
 ROW_TILES = 4
 UNIT = P * ROW_TILES
-CHUNKS = B // UNIT
+PAIR = 2
 RUN = 2
+
+FIRST_SIZES = [2, 2] + [ROW_TILES] * 7
+INNER_SIZES = [ROW_TILES] * 8
+LAST_SIZES = [ROW_TILES] * 7 + [2, 1, 1]
+
+SHARED_UNITS = [2, 4, 6]
 
 FLOPS = 2 * B * G * (H * H + H * PD)
 
@@ -31,7 +37,7 @@ def tile_linearwdecoder_pb_t_kernel(tc, h, W3, b3, Wo, bo, out):
         grouped_pool = ctx.enter_context(tc.tile_pool(name="grouped", bufs=5))
         mx_pool = ctx.enter_context(tc.tile_pool(name="mx", bufs=3))
         relu_pool = ctx.enter_context(tc.tile_pool(name="relu", bufs=3))
-        h3_pool = ctx.enter_context(tc.tile_pool(name="h3", bufs=2))
+        h3_pool = ctx.enter_context(tc.tile_pool(name="h3", bufs=3))
         result_pool = ctx.enter_context(tc.tile_pool(name="result", bufs=3))
         turned_pool = ctx.enter_context(tc.psum_pool(name="turned", bufs=2))
         hidden_pool = ctx.enter_context(tc.psum_pool(name="hidden", bufs=PACK))
@@ -39,43 +45,58 @@ def tile_linearwdecoder_pb_t_kernel(tc, h, W3, b3, Wo, bo, out):
 
         identity = const.tile([P, P], F32)
         make_identity(nc, identity[:])
+        identity_bf16 = const.tile([P, P], BF16)
+        make_identity(nc, identity_bf16[:])
 
-        h_units = h.rearrange("(c p i) g k -> c g p i k", p=P, i=ROW_TILES)
-        out_units = out.rearrange("(c p i) (g n) -> c g p i n", p=P, i=ROW_TILES, g=G)
-        w3_units = W3.rearrange("g (p t) k -> g p t k", t=PACK)
-
-        stream = [(Wo.rearrange("g p k -> p g k"), None, None)]
-        w3_place = []
+        stream = []
+        w3_place = {}
+        wo_place = 0
         for g in range(G):
-            w3_place.append(len(stream))
-            stream.append((w3_units[g], g, None))
-            for c in range(CHUNKS):
-                stream.append((h_units[c, g], g, c))
+            w3_place[g] = len(stream)
+            stream.append(("w3", g, None, ROW_TILES, [nc.scalar, nc.vector] if g == 0 else [nc.scalar, nc.scalar]))
+            sizes = FIRST_SIZES if g == 0 else LAST_SIZES if g == G - 1 else INNER_SIZES
+            token = 0
+            for k, size in enumerate(sizes):
+                if g == 0 and k == 2:
+                    wo_place = len(stream)
+                    stream.append(("wo", None, None, ROW_TILES, [nc.scalar, nc.scalar]))
+                first_tokens = g == 0 and k == 0
+                stream.append(("tokens", g, token, size, [nc.vector if first_tokens else nc.scalar] * PAIR))
+                token += P * size
+        shared = [n for n, unit in enumerate(stream) if unit[0] == "tokens" and unit[3] == ROW_TILES and unit[2] // UNIT in SHARED_UNITS]
         tiles = {}
 
         def in_stream(n):
             return 0 <= n < len(stream)
 
         def is_tokens(n):
-            return in_stream(n) and stream[n][2] is not None
+            return in_stream(n) and stream[n][0] == "tokens"
 
         def is_w3(n):
-            return in_stream(n) and stream[n][1] is not None and stream[n][2] is None
+            return in_stream(n) and stream[n][0] == "w3"
+
+        def rows_in_dram(n):
+            kind, g, token, size = stream[n][:4]
+            if kind == "tokens":
+                return h[token : token + P * size, g, :].rearrange("(p i) k -> p i k", i=size)
+            if kind == "w3":
+                return W3[g].rearrange("(p t) k -> p t k", t=PACK)
+            return Wo.rearrange("g p k -> p g k")
 
         def load(n):
             if not in_stream(n):
                 return
-            view = stream[n][0]
-            rows = rows_pool.tile([P, UNIT * PACK], BF16)
-            nc.sync.dma_start(out=rows[:].rearrange("p (i k) -> p i k", i=view.shape[1]), in_=view)
+            size = stream[n][3]
+            rows = rows_pool.tile([P, ROW_TILES, H], BF16)
+            view = rows_in_dram(n)
+            step = PAIR if n == 0 else size
+            for i in range(0, size, step):
+                nc.sync.dma_start(out=rows[:, i : i + step, :], in_=view[:, i : i + step, :])
             tiles["rows", n] = rows
             if is_w3(n):
                 g = stream[n][1]
                 b3_pairs = weights.tile([P, PACK], BF16)
-                nc.scalar.dma_start(
-                    out=b3_pairs[:],
-                    in_=b3[g].rearrange("(p t) -> p t", t=PACK),
-                )
+                nc.scalar.dma_start(out=b3_pairs[:], in_=b3[g].rearrange("(p t) -> p t", t=PACK))
                 bo_rows = weights.tile([P, PD], BF16)
                 nc.scalar.dma_start(out=bo_rows[:], in_=bo[g].partition_broadcast(P))
                 tiles["b3_pairs", g] = b3_pairs
@@ -84,36 +105,44 @@ def tile_linearwdecoder_pb_t_kernel(tc, h, W3, b3, Wo, bo, out):
         def turn(n):
             if not in_stream(n):
                 return
-            row_words = tiles["rows", n][:].bitcast(F32)
-            for pair in range(ROW_TILES // 2):
-                turned = turned_pool.tile([P, 2, 2 * P], F32)
-                for j in range(2):
-                    for u in range(2):
-                        first = (2 * pair + j) * 2 * P
-                        nc.tensor.transpose(
-                            turned[:, u, j * P : (j + 1) * P], row_words[:, first + u : first + 2 * P : 2], identity[:]
-                        )
-                tiles["turned", n, pair] = turned
+            for i in range(stream[n][3]):
+                if i % PAIR == 0:
+                    turned = turned_pool.tile([P, 2, PAIR * P], F32)
+                    tiles["turned", n, i // PAIR] = turned
+                words = tiles["rows", n][:, i, :].bitcast(F32)
+                j = i % PAIR
+                for u in range(2):
+                    nc.tensor.transpose(turned[:, u, j * P : (j + 1) * P], words[:, u : 2 * P : 2], identity[:])
 
         def regroup(n):
             if not in_stream(n):
                 return
+            size, engines = stream[n][3], stream[n][4]
             grouped = grouped_pool.tile([P, UNIT * PACK], BF16, align_bytes=64)
             grouped_words = grouped[:].bitcast(F32).rearrange("p (c u) -> p c u", u=2)
-            for pair in range(ROW_TILES // 2):
-                nc.scalar.copy(
-                    out=grouped_words[:, pair * 2 * P : (pair + 1) * 2 * P, :],
-                    in_=tiles["turned", n, pair][:].rearrange("p u c -> p c u"),
+            for i in range(0, size, PAIR):
+                columns = slice(i * P, min(i + PAIR, size) * P)
+                width = columns.stop - columns.start
+                engine = engines[i // PAIR]
+                copy = engine.copy if engine is nc.scalar else engine.tensor_copy
+                copy(
+                    out=grouped_words[:, columns, :],
+                    in_=tiles["turned", n, i // PAIR][:, :, :width].rearrange("p u c -> p c u"),
                 )
             tiles["grouped", n] = grouped
 
         def quantise(n):
             if not in_stream(n):
                 return
+            columns = P * stream[n][3]
             pool = mx_pool if is_tokens(n) else weights
             codes = pool.tile([P, UNIT], U32, align_bytes=64)
             scales = pool.tile([P, UNIT], U8, align_bytes=64)
-            nc.vector.quantize_mx(out=codes[:].bitcast(FP8X4), scales=scales[:], in_=tiles["grouped", n][:])
+            nc.vector.quantize_mx(
+                out=codes[:, :columns].bitcast(FP8X4),
+                scales=scales[:, :columns],
+                in_=tiles["grouped", n][:, : columns * PACK],
+            )
             tiles["codes", n] = codes
             tiles["scales", n] = scales
             if is_w3(n):
@@ -126,14 +155,15 @@ def tile_linearwdecoder_pb_t_kernel(tc, h, W3, b3, Wo, bo, out):
             if not is_tokens(n):
                 return
             w3 = w3_place[stream[n][1]]
+            columns = P * stream[n][3]
             for t in range(PACK):
                 hidden = hidden_pool.tile([P, UNIT], F32)
                 nc.tensor.matmul_mx(
-                    out=hidden[:],
+                    out=hidden[:, :columns],
                     lhsT=tiles["codes", w3][:, t * P : (t + 1) * P].bitcast(FP8X4),
                     lhsT_scale=tiles["scales", w3][:, t * P : (t + 1) * P],
-                    rhs=tiles["codes", n][:].bitcast(FP8X4),
-                    rhs_scale=tiles["scales", n][:],
+                    rhs=tiles["codes", n][:, :columns].bitcast(FP8X4),
+                    rhs_scale=tiles["scales", n][:, :columns],
                     start=True,
                     stop=True,
                 )
@@ -143,24 +173,49 @@ def tile_linearwdecoder_pb_t_kernel(tc, h, W3, b3, Wo, bo, out):
             if not is_tokens(n):
                 return
             g = stream[n][1]
+            columns = P * stream[n][3]
             relu = relu_pool.tile([P, PACK, UNIT], F32)
             for t in range(PACK):
                 nc.scalar.activation(
-                    out=relu[:, t, :],
-                    in_=tiles["hidden", n, t][:],
+                    out=relu[:, t, :columns],
+                    in_=tiles["hidden", n, t][:, :columns],
                     func=RELU,
                     bias=tiles["b3_columns", g][:, t : t + 1],
                 )
             tiles["relu", n] = relu
 
+        def add_on_tensor(n):
+            if n not in shared:
+                return
+            last = slice((ROW_TILES - 1) * P, UNIT)
+            h_values = tiles["grouped", n][:].rearrange("p (c t) -> p c t", t=PACK)
+            projected = projected_pool.tile([P, ROW_TILES, PD], F32)
+            for t in range(PACK):
+                nc.tensor.matmul(
+                    projected[:, t, :], lhsT=identity[:], rhs=tiles["relu", n][:, t, last], start=True, stop=False
+                )
+                nc.tensor.matmul(
+                    projected[:, t, :], lhsT=identity_bf16[:], rhs=h_values[:, last, t], start=False, stop=True
+                )
+            tiles["sums", n] = projected
+
+        def round_sums(n):
+            if n not in shared:
+                return
+            nc.scalar.copy(
+                out=tiles["h3", n][:, (ROW_TILES - 1) * P * PACK :].rearrange("p (c t) -> p c t", t=PACK),
+                in_=tiles["sums", n][:].rearrange("p t c -> p c t"),
+            )
+
         def add_residual(n):
             if not is_tokens(n):
                 return
+            columns = P * (stream[n][3] - (1 if n in shared else 0))
             h3 = h3_pool.tile([P, UNIT * PACK], BF16, align_bytes=64)
             nc.vector.tensor_tensor(
-                out=h3[:].rearrange("p (c i t) -> p c t i", i=RUN, t=PACK),
-                in0=tiles["relu", n][:].rearrange("p t (c i) -> p c t i", i=RUN),
-                in1=tiles["grouped", n][:].rearrange("p (c i t) -> p c t i", i=RUN, t=PACK),
+                out=h3[:, : columns * PACK].rearrange("p (c i t) -> p c t i", i=RUN, t=PACK),
+                in0=tiles["relu", n][:, :, :columns].rearrange("p t (c i) -> p c t i", i=RUN),
+                in1=tiles["grouped", n][:, : columns * PACK].rearrange("p (c i t) -> p c t i", i=RUN, t=PACK),
                 op=ADD,
             )
             tiles["h3", n] = h3
@@ -168,9 +223,14 @@ def tile_linearwdecoder_pb_t_kernel(tc, h, W3, b3, Wo, bo, out):
         def quantise_h3(n):
             if not is_tokens(n):
                 return
+            columns = P * stream[n][3]
             h3_codes = h3_pool.tile([P, UNIT], U32, align_bytes=64)
             h3_scales = h3_pool.tile([P, UNIT], U8, align_bytes=64)
-            nc.vector.quantize_mx(out=h3_codes[:].bitcast(FP8X4), scales=h3_scales[:], in_=tiles["h3", n][:])
+            nc.vector.quantize_mx(
+                out=h3_codes[:, :columns].bitcast(FP8X4),
+                scales=h3_scales[:, :columns],
+                in_=tiles["h3", n][:, : columns * PACK],
+            )
             tiles["h3_codes", n] = h3_codes
             tiles["h3_scales", n] = h3_scales
 
@@ -179,13 +239,13 @@ def tile_linearwdecoder_pb_t_kernel(tc, h, W3, b3, Wo, bo, out):
                 return
             g = stream[n][1]
             projected = projected_pool.tile([P, ROW_TILES, PD], F32)
-            for i in range(ROW_TILES):
+            for i in range(stream[n][3]):
                 nc.tensor.matmul_mx(
                     out=projected[:, i, :],
                     lhsT=tiles["h3_codes", n][:, i * P : (i + 1) * P].bitcast(FP8X4),
                     lhsT_scale=tiles["h3_scales", n][:, i * P : (i + 1) * P],
-                    rhs=tiles["codes", 0][:, g * PD : (g + 1) * PD].bitcast(FP8X4),
-                    rhs_scale=tiles["scales", 0][:, g * PD : (g + 1) * PD],
+                    rhs=tiles["codes", wo_place][:, g * PD : (g + 1) * PD].bitcast(FP8X4),
+                    rhs_scale=tiles["scales", wo_place][:, g * PD : (g + 1) * PD],
                     start=True,
                     stop=True,
                 )
@@ -194,25 +254,28 @@ def tile_linearwdecoder_pb_t_kernel(tc, h, W3, b3, Wo, bo, out):
         def finish(n):
             if not is_tokens(n):
                 return
-            g, c = stream[n][1], stream[n][2]
+            g, token, size = stream[n][1:4]
             result = result_pool.tile([P, ROW_TILES, PD], F32)
             nc.vector.tensor_tensor(
-                out=result[:],
-                in0=tiles["projected", n][:],
-                in1=tiles["bo_rows", g][:].unsqueeze(1).to_broadcast([P, ROW_TILES, PD]),
+                out=result[:, :size, :],
+                in0=tiles["projected", n][:, :size, :],
+                in1=tiles["bo_rows", g][:].unsqueeze(1).to_broadcast([P, size, PD]),
                 op=ADD,
             )
-            nc.sync.dma_start(out=out_units[c, g], in_=result[:])
+            rows = out[token : token + P * size, g * PD : (g + 1) * PD]
+            nc.sync.dma_start(out=rows.rearrange("(p i) n -> p i n", i=size), in_=result[:, :size, :])
 
         with tc.manual_schedule():
-            for step in range(len(stream) + 7):
+            for step in range(len(stream) + 8):
                 load(step)
-                quantise(step - 4)
+                regroup(step - 4)
+                multiply_wo(step - 8)
                 turn(step - 3)
-                multiply_wo(step - 7)
+                add_on_tensor(step - 6)
                 bias_relu(step - 5)
-                multiply_w3(step - 4)
-                regroup(step - 3)
                 add_residual(step - 6)
-                finish(step - 7)
-                quantise_h3(step - 6)
+                round_sums(step - 6)
+                quantise(step - 4)
+                multiply_w3(step - 4)
+                quantise_h3(step - 7)
+                finish(step - 8)

@@ -23,8 +23,6 @@ FIRST_SIZES = [2, 2] + [ROW_TILES] * 7
 INNER_SIZES = [ROW_TILES] * 8
 LAST_SIZES = [ROW_TILES] * 7 + [2, 1, 1]
 
-SHARED_UNITS = [2, 4, 6]
-
 FLOPS = 2 * B * G * (H * H + H * PD)
 
 
@@ -34,7 +32,7 @@ def tile_linearwdecoder_pb_t_kernel(tc, h, W3, b3, Wo, bo, out):
         const = ctx.enter_context(tc.tile_pool(name="const", bufs=1))
         weights = ctx.enter_context(tc.tile_pool(name="weights", bufs=G + 1))
         rows_pool = ctx.enter_context(tc.tile_pool(name="rows", bufs=6))
-        grouped_pool = ctx.enter_context(tc.tile_pool(name="grouped", bufs=5))
+        grouped_pool = ctx.enter_context(tc.tile_pool(name="grouped", bufs=6))
         mx_pool = ctx.enter_context(tc.tile_pool(name="mx", bufs=3))
         relu_pool = ctx.enter_context(tc.tile_pool(name="relu", bufs=3))
         h3_pool = ctx.enter_context(tc.tile_pool(name="h3", bufs=3))
@@ -45,8 +43,6 @@ def tile_linearwdecoder_pb_t_kernel(tc, h, W3, b3, Wo, bo, out):
 
         identity = const.tile([P, P], F32)
         make_identity(nc, identity[:])
-        identity_bf16 = const.tile([P, P], BF16)
-        make_identity(nc, identity_bf16[:])
 
         stream = []
         w3_place = {}
@@ -63,7 +59,6 @@ def tile_linearwdecoder_pb_t_kernel(tc, h, W3, b3, Wo, bo, out):
                 first_tokens = g == 0 and k == 0
                 stream.append(("tokens", g, token, size, [nc.vector if first_tokens else nc.scalar] * PAIR))
                 token += P * size
-        shared = [n for n, unit in enumerate(stream) if unit[0] == "tokens" and unit[3] == ROW_TILES and unit[2] // UNIT in SHARED_UNITS]
         tiles = {}
 
         def in_stream(n):
@@ -102,34 +97,32 @@ def tile_linearwdecoder_pb_t_kernel(tc, h, W3, b3, Wo, bo, out):
                 tiles["b3_pairs", g] = b3_pairs
                 tiles["bo_rows", g] = bo_rows
 
-        def turn(n):
-            if not in_stream(n):
+        def turn(n, pair):
+            if not in_stream(n) or pair * PAIR >= stream[n][3]:
                 return
-            for i in range(stream[n][3]):
-                if i % PAIR == 0:
-                    turned = turned_pool.tile([P, 2, PAIR * P], F32)
-                    tiles["turned", n, i // PAIR] = turned
+            turned = turned_pool.tile([P, 2, PAIR * P], F32)
+            tiles["turned", n, pair] = turned
+            for i in range(pair * PAIR, min((pair + 1) * PAIR, stream[n][3])):
                 words = tiles["rows", n][:, i, :].bitcast(F32)
                 j = i % PAIR
                 for u in range(2):
                     nc.tensor.transpose(turned[:, u, j * P : (j + 1) * P], words[:, u : 2 * P : 2], identity[:])
 
-        def regroup(n):
-            if not in_stream(n):
+        def regroup(n, pair):
+            if not in_stream(n) or pair * PAIR >= stream[n][3]:
                 return
-            size, engines = stream[n][3], stream[n][4]
-            grouped = grouped_pool.tile([P, UNIT * PACK], BF16, align_bytes=64)
-            grouped_words = grouped[:].bitcast(F32).rearrange("p (c u) -> p c u", u=2)
-            for i in range(0, size, PAIR):
-                columns = slice(i * P, min(i + PAIR, size) * P)
-                width = columns.stop - columns.start
-                engine = engines[i // PAIR]
-                copy = engine.copy if engine is nc.scalar else engine.tensor_copy
-                copy(
-                    out=grouped_words[:, columns, :],
-                    in_=tiles["turned", n, i // PAIR][:, :, :width].rearrange("p u c -> p c u"),
-                )
-            tiles["grouped", n] = grouped
+            if pair == 0:
+                grouped = grouped_pool.tile([P, UNIT * PACK], BF16, align_bytes=64)
+                tiles["grouped", n] = grouped
+            grouped_words = tiles["grouped", n][:].bitcast(F32).rearrange("p (c u) -> p c u", u=2)
+            columns = slice(pair * PAIR * P, min((pair + 1) * PAIR, stream[n][3]) * P)
+            width = columns.stop - columns.start
+            engine = stream[n][4][pair]
+            copy = engine.copy if engine is nc.scalar else engine.tensor_copy
+            copy(
+                out=grouped_words[:, columns, :],
+                in_=tiles["turned", n, pair][:, :, :width].rearrange("p u c -> p c u"),
+            )
 
         def quantise(n):
             if not in_stream(n):
@@ -151,12 +144,12 @@ def tile_linearwdecoder_pb_t_kernel(tc, h, W3, b3, Wo, bo, out):
                 nc.vector.tensor_copy(out=b3_columns[:], in_=tiles["b3_pairs", g][:])
                 tiles["b3_columns", g] = b3_columns
 
-        def multiply_w3(n):
+        def multiply_w3(n, ts):
             if not is_tokens(n):
                 return
             w3 = w3_place[stream[n][1]]
             columns = P * stream[n][3]
-            for t in range(PACK):
+            for t in ts:
                 hidden = hidden_pool.tile([P, UNIT], F32)
                 nc.tensor.matmul_mx(
                     out=hidden[:, :columns],
@@ -169,48 +162,26 @@ def tile_linearwdecoder_pb_t_kernel(tc, h, W3, b3, Wo, bo, out):
                 )
                 tiles["hidden", n, t] = hidden
 
-        def bias_relu(n):
+        def bias_relu(n, ts):
             if not is_tokens(n):
                 return
             g = stream[n][1]
             columns = P * stream[n][3]
-            relu = relu_pool.tile([P, PACK, UNIT], F32)
-            for t in range(PACK):
+            if ts[0] == 0:
+                relu = relu_pool.tile([P, PACK, UNIT], F32)
+                tiles["relu", n] = relu
+            for t in ts:
                 nc.scalar.activation(
-                    out=relu[:, t, :columns],
+                    out=tiles["relu", n][:, t, :columns],
                     in_=tiles["hidden", n, t][:, :columns],
                     func=RELU,
                     bias=tiles["b3_columns", g][:, t : t + 1],
                 )
-            tiles["relu", n] = relu
-
-        def add_on_tensor(n):
-            if n not in shared:
-                return
-            last = slice((ROW_TILES - 1) * P, UNIT)
-            h_values = tiles["grouped", n][:].rearrange("p (c t) -> p c t", t=PACK)
-            projected = projected_pool.tile([P, ROW_TILES, PD], F32)
-            for t in range(PACK):
-                nc.tensor.matmul(
-                    projected[:, t, :], lhsT=identity[:], rhs=tiles["relu", n][:, t, last], start=True, stop=False
-                )
-                nc.tensor.matmul(
-                    projected[:, t, :], lhsT=identity_bf16[:], rhs=h_values[:, last, t], start=False, stop=True
-                )
-            tiles["sums", n] = projected
-
-        def round_sums(n):
-            if n not in shared:
-                return
-            nc.scalar.copy(
-                out=tiles["h3", n][:, (ROW_TILES - 1) * P * PACK :].rearrange("p (c t) -> p c t", t=PACK),
-                in_=tiles["sums", n][:].rearrange("p t c -> p c t"),
-            )
 
         def add_residual(n):
             if not is_tokens(n):
                 return
-            columns = P * (stream[n][3] - (1 if n in shared else 0))
+            columns = P * stream[n][3]
             h3 = h3_pool.tile([P, UNIT * PACK], BF16, align_bytes=64)
             nc.vector.tensor_tensor(
                 out=h3[:, : columns * PACK].rearrange("p (c i t) -> p c t i", i=RUN, t=PACK),
@@ -265,17 +236,20 @@ def tile_linearwdecoder_pb_t_kernel(tc, h, W3, b3, Wo, bo, out):
             rows = out[token : token + P * size, g * PD : (g + 1) * PD]
             nc.sync.dma_start(out=rows.rearrange("(p i) n -> p i n", i=size), in_=result[:, :size, :])
 
+        first_half, second_half = [0, 1], [2, 3]
         with tc.manual_schedule():
-            for step in range(len(stream) + 8):
+            for step in range(len(stream) + 9):
                 load(step)
-                regroup(step - 4)
-                multiply_wo(step - 8)
-                turn(step - 3)
-                add_on_tensor(step - 6)
-                bias_relu(step - 5)
-                add_residual(step - 6)
-                round_sums(step - 6)
+                regroup(step - 4, 0)
+                multiply_wo(step - 9)
+                turn(step - 3, 0)
+                bias_relu(step - 6, first_half)
+                multiply_w3(step - 5, first_half)
+                regroup(step - 4, 1)
+                turn(step - 3, 1)
+                bias_relu(step - 6, second_half)
+                multiply_w3(step - 5, second_half)
+                add_residual(step - 7)
+                quantise_h3(step - 8)
                 quantise(step - 4)
-                multiply_w3(step - 4)
-                quantise_h3(step - 7)
-                finish(step - 8)
+                finish(step - 9)

@@ -23,6 +23,8 @@ FIRST_SIZES = [2, 2] + [ROW_TILES] * 7
 INNER_SIZES = [ROW_TILES] * 8
 LAST_SIZES = [ROW_TILES] * 7 + [2, 1, 1]
 
+SHARED_UNITS = [2, 4, 6]
+
 FLOPS = 2 * B * G * (H * H + H * PD)
 
 
@@ -34,7 +36,7 @@ def tile_linearwdecoder_pb_t_kernel(tc, h, W3, b3, Wo, bo, out):
         rows_pool = ctx.enter_context(tc.tile_pool(name="rows", bufs=6))
         grouped_pool = ctx.enter_context(tc.tile_pool(name="grouped", bufs=6))
         mx_pool = ctx.enter_context(tc.tile_pool(name="mx", bufs=3))
-        relu_pool = ctx.enter_context(tc.tile_pool(name="relu", bufs=3))
+        relu_pool = ctx.enter_context(tc.tile_pool(name="relu", bufs=4))
         h3_pool = ctx.enter_context(tc.tile_pool(name="h3", bufs=3))
         result_pool = ctx.enter_context(tc.tile_pool(name="result", bufs=3))
         turned_pool = ctx.enter_context(tc.psum_pool(name="turned", bufs=2))
@@ -43,6 +45,8 @@ def tile_linearwdecoder_pb_t_kernel(tc, h, W3, b3, Wo, bo, out):
 
         identity = const.tile([P, P], F32)
         make_identity(nc, identity[:])
+        identity_bf16 = const.tile([P, P], BF16)
+        make_identity(nc, identity_bf16[:])
 
         stream = []
         w3_place = {}
@@ -59,6 +63,11 @@ def tile_linearwdecoder_pb_t_kernel(tc, h, W3, b3, Wo, bo, out):
                 first_tokens = g == 0 and k == 0
                 stream.append(("tokens", g, token, size, [nc.vector if first_tokens else nc.scalar] * PAIR))
                 token += P * size
+        shared = [
+            n
+            for n, (kind, code, token, size, engines) in enumerate(stream)
+            if kind == "tokens" and size == ROW_TILES and token // UNIT in SHARED_UNITS
+        ]
         tiles = {}
 
         def in_stream(n):
@@ -178,10 +187,33 @@ def tile_linearwdecoder_pb_t_kernel(tc, h, W3, b3, Wo, bo, out):
                     bias=tiles["b3_columns", g][:, t : t + 1],
                 )
 
+        def add_on_tensor(n):
+            if n not in shared:
+                return
+            last = slice((ROW_TILES - 1) * P, UNIT)
+            h_values = tiles["grouped", n][:].rearrange("p (c t) -> p c t", t=PACK)
+            projected = projected_pool.tile([P, ROW_TILES, PD], F32)
+            for t in range(PACK):
+                nc.tensor.matmul(
+                    projected[:, t, :], lhsT=identity[:], rhs=tiles["relu", n][:, t, last], start=True, stop=False
+                )
+                nc.tensor.matmul(
+                    projected[:, t, :], lhsT=identity_bf16[:], rhs=h_values[:, last, t], start=False, stop=True
+                )
+            tiles["sums", n] = projected
+
+        def round_sums(n):
+            if n not in shared:
+                return
+            nc.scalar.copy(
+                out=tiles["h3", n][:, (ROW_TILES - 1) * P * PACK :].rearrange("p (c t) -> p c t", t=PACK),
+                in_=tiles["sums", n][:].rearrange("p t c -> p c t"),
+            )
+
         def add_residual(n):
             if not is_tokens(n):
                 return
-            columns = P * stream[n][3]
+            columns = P * (stream[n][3] - (1 if n in shared else 0))
             h3 = h3_pool.tile([P, UNIT * PACK], BF16, align_bytes=64)
             nc.vector.tensor_tensor(
                 out=h3[:, : columns * PACK].rearrange("p (c i t) -> p c t i", i=RUN, t=PACK),
@@ -241,10 +273,12 @@ def tile_linearwdecoder_pb_t_kernel(tc, h, W3, b3, Wo, bo, out):
             for step in range(len(stream) + 9):
                 load(step)
                 regroup(step - 4, 0)
-                multiply_wo(step - 9)
+                round_sums(step - 8)
                 turn(step - 3, 0)
+                multiply_wo(step - 9)
                 bias_relu(step - 6, first_half)
                 multiply_w3(step - 5, first_half)
+                add_on_tensor(step - 7)
                 regroup(step - 4, 1)
                 turn(step - 3, 1)
                 bias_relu(step - 6, second_half)

@@ -19,11 +19,19 @@ UNIT = P * ROW_TILES
 PAIR = 2
 RUN = 2
 
-FIRST_SIZES = [2, 2] + [ROW_TILES] * 7
+FIRST_SIZES = [1, 1, 2, 2, 2, 4, 4, 4, 4, 4, 4]
 INNER_SIZES = [ROW_TILES] * 8
-LAST_SIZES = [ROW_TILES] * 7 + [2, 1, 1]
+LAST_SIZES = [4, 4, 4, 4, 4, 4, 4, 2, 1, 1]
 
-SHARED_UNITS = [2, 4, 6]
+SHARED_FROM = 1
+SHARED_UNITS = [3, 6]
+
+QUANTISE_H = 4
+QUANTISE_H3 = 8
+W3_AHEAD = 4
+WO_STEP = 5
+REGROUP_ON_VECTOR = [(3, 0), (4, 0), (5, 1), (6, 1)]
+HEAD_UNITS = 2
 
 FLOPS = 2 * B * G * (H * H + H * PD)
 
@@ -32,12 +40,12 @@ def tile_linearwdecoder_pb_t_kernel(tc, h, W3, b3, Wo, bo, out):
     nc = tc.nc
     with ExitStack() as ctx:
         const = ctx.enter_context(tc.tile_pool(name="const", bufs=1))
+        weights_pool = ctx.enter_context(tc.tile_pool(name="weights_pool", bufs=2))
         weights = ctx.enter_context(tc.tile_pool(name="weights", bufs=G + 1))
-        rows_pool = ctx.enter_context(tc.tile_pool(name="rows", bufs=6))
-        grouped_pool = ctx.enter_context(tc.tile_pool(name="grouped", bufs=6))
+        rows_pool = ctx.enter_context(tc.tile_pool(name="rows", bufs=7))
+        values_pool = ctx.enter_context(tc.tile_pool(name="values", bufs=8))
         mx_pool = ctx.enter_context(tc.tile_pool(name="mx", bufs=3))
         relu_pool = ctx.enter_context(tc.tile_pool(name="relu", bufs=4))
-        h3_pool = ctx.enter_context(tc.tile_pool(name="h3", bufs=3))
         result_pool = ctx.enter_context(tc.tile_pool(name="result", bufs=3))
         turned_pool = ctx.enter_context(tc.psum_pool(name="turned", bufs=2))
         hidden_pool = ctx.enter_context(tc.psum_pool(name="hidden", bufs=PACK))
@@ -48,116 +56,168 @@ def tile_linearwdecoder_pb_t_kernel(tc, h, W3, b3, Wo, bo, out):
         identity_bf16 = const.tile([P, P], BF16)
         make_identity(nc, identity_bf16[:])
 
-        stream = []
-        w3_place = {}
-        wo_place = 0
+        units = []
+        first_of = []
         for g in range(G):
-            w3_place[g] = len(stream)
-            stream.append(("w3", g, None, ROW_TILES, [nc.scalar, nc.vector] if g == 0 else [nc.scalar, nc.scalar]))
+            first_of.append(len(units))
             sizes = FIRST_SIZES if g == 0 else LAST_SIZES if g == G - 1 else INNER_SIZES
             token = 0
-            for k, size in enumerate(sizes):
-                if g == 0 and k == 2:
-                    wo_place = len(stream)
-                    stream.append(("wo", None, None, ROW_TILES, [nc.scalar, nc.scalar]))
-                first_tokens = g == 0 and k == 0
-                stream.append(("tokens", g, token, size, [nc.vector if first_tokens else nc.scalar] * PAIR))
+            for size in sizes:
+                units.append((g, token, size))
                 token += P * size
-        shared = [
-            n
-            for n, (kind, code, token, size, engines) in enumerate(stream)
-            if kind == "tokens" and size == ROW_TILES and token // UNIT in SHARED_UNITS
-        ]
+        shared = [n for n, (g, token, size) in enumerate(units) if size == ROW_TILES and g >= SHARED_FROM and token // UNIT in SHARED_UNITS]
+        weight_steps = {WO_STEP: "wo"}
+        for g in range(1, G):
+            weight_steps[first_of[g] + QUANTISE_H - W3_AHEAD] = g
         tiles = {}
 
-        def in_stream(n):
-            return 0 <= n < len(stream)
+        def is_unit(n):
+            return 0 <= n < len(units)
 
-        def is_tokens(n):
-            return in_stream(n) and stream[n][0] == "tokens"
-
-        def is_w3(n):
-            return in_stream(n) and stream[n][0] == "w3"
-
-        def rows_in_dram(n):
-            kind, g, token, size = stream[n][:4]
-            if kind == "tokens":
-                return h[token : token + P * size, g, :].rearrange("(p i) k -> p i k", i=size)
-            if kind == "w3":
-                return W3[g].rearrange("(p t) k -> p t k", t=PACK)
-            return Wo.rearrange("g p k -> p g k")
-
-        def load(n):
-            if not in_stream(n):
-                return
-            size = stream[n][3]
+        def load_rows(key, view, size, step):
             rows = rows_pool.tile([P, ROW_TILES, H], BF16)
-            view = rows_in_dram(n)
-            step = PAIR if n == 0 else size
             for i in range(0, size, step):
                 nc.sync.dma_start(out=rows[:, i : i + step, :], in_=view[:, i : i + step, :])
-            tiles["rows", n] = rows
-            if is_w3(n):
-                g = stream[n][1]
-                b3_pairs = weights.tile([P, PACK], BF16)
-                nc.scalar.dma_start(out=b3_pairs[:], in_=b3[g].rearrange("(p t) -> p t", t=PACK))
-                bo_rows = weights.tile([P, PD], BF16)
-                nc.scalar.dma_start(out=bo_rows[:], in_=bo[g].partition_broadcast(P))
-                tiles["b3_pairs", g] = b3_pairs
-                tiles["bo_rows", g] = bo_rows
+            tiles["rows", key] = rows
 
-        def turn(n, pair):
-            if not in_stream(n) or pair * PAIR >= stream[n][3]:
+        def load_weights(w, step):
+            if w == "wo":
+                load_rows(w, Wo.rearrange("g p k -> p g k"), ROW_TILES, step)
                 return
-            turned = turned_pool.tile([P, 2, PAIR * P], F32)
-            tiles["turned", n, pair] = turned
-            for i in range(pair * PAIR, min((pair + 1) * PAIR, stream[n][3])):
-                words = tiles["rows", n][:, i, :].bitcast(F32)
+            load_rows(("w3", w), W3[w].rearrange("(p t) k -> p t k", t=PACK), ROW_TILES, step)
+            b3_pairs = weights.tile([P, PACK], BF16)
+            nc.scalar.dma_start(out=b3_pairs[:], in_=b3[w].rearrange("(p t) -> p t", t=PACK))
+            tiles["b3_pairs", w] = b3_pairs
+
+        def load_bo(g):
+            bo_rows = weights.tile([P, PD], BF16)
+            nc.sync.dma_start(out=bo_rows[:], in_=bo[g].partition_broadcast(P))
+            tiles["bo_rows", g] = bo_rows
+
+        def load(n):
+            if is_unit(n):
+                g, token, size = units[n]
+                load_rows(n, h[token : token + P * size, g, :].rearrange("(p i) k -> p i k", i=size), size, size)
+
+        def turn(key, size, pair, bank=None):
+            if pair * PAIR >= size:
+                return
+            if bank is None:
+                turned = turned_pool.tile([P, 2, PAIR * P], F32)
+            else:
+                turned = projected_pool.tile([P, 2, PAIR * P], F32, tag="projected", name="projected")
+            tiles["turned", key, pair] = turned
+            for i in range(pair * PAIR, min((pair + 1) * PAIR, size)):
+                words = tiles["rows", key][:, i, :].bitcast(F32)
                 j = i % PAIR
                 for u in range(2):
                     nc.tensor.transpose(turned[:, u, j * P : (j + 1) * P], words[:, u : 2 * P : 2], identity[:])
 
-        def regroup(n, pair):
-            if not in_stream(n) or pair * PAIR >= stream[n][3]:
+        def turn_unit(n, pair):
+            if is_unit(n):
+                turn(n, units[n][2], pair)
+
+        def values_of(step):
+            if ("values", step) not in tiles:
+                values = values_pool.tile([P, 2 * UNIT * PACK], BF16, align_bytes=64)
+                tiles["values", step] = values
+            return tiles["values", step]
+
+        def regroup(key, size, pair, engine):
+            if pair * PAIR >= size:
                 return
-            if pair == 0:
-                grouped = grouped_pool.tile([P, UNIT * PACK], BF16, align_bytes=64)
-                tiles["grouped", n] = grouped
-            grouped_words = tiles["grouped", n][:].bitcast(F32).rearrange("p (c u) -> p c u", u=2)
-            columns = slice(pair * PAIR * P, min((pair + 1) * PAIR, stream[n][3]) * P)
+            grouped_words = tiles["grouped", key].bitcast(F32).rearrange("p (c u) -> p c u", u=2)
+            columns = slice(pair * PAIR * P, min((pair + 1) * PAIR, size) * P)
             width = columns.stop - columns.start
-            engine = stream[n][4][pair]
             copy = engine.copy if engine is nc.scalar else engine.tensor_copy
             copy(
                 out=grouped_words[:, columns, :],
-                in_=tiles["turned", n, pair][:, :, :width].rearrange("p u c -> p c u"),
+                in_=tiles["turned", key, pair][:, :, :width].rearrange("p u c -> p c u"),
             )
 
-        def quantise(n):
-            if not in_stream(n):
-                return
-            columns = P * stream[n][3]
-            pool = mx_pool if is_tokens(n) else weights
-            codes = pool.tile([P, UNIT], U32, align_bytes=64)
-            scales = pool.tile([P, UNIT], U8, align_bytes=64)
+        def regroup_unit(n, pair, engine=nc.scalar):
+            if is_unit(n):
+                if pair == 0:
+                    tiles["grouped", n] = values_of(n + QUANTISE_H)[:, : UNIT * PACK]
+                regroup(n, units[n][2], pair, nc.vector if (n, pair) in REGROUP_ON_VECTOR else engine)
+
+        def regroup_weights(key, pair, engine):
+            if pair == 0:
+                w_grouped = weights_pool.tile([P, UNIT * PACK], BF16, align_bytes=64)
+                tiles["grouped", key] = w_grouped[:]
+            regroup(key, ROW_TILES, pair, engine)
+
+        def quantise_columns(codes, scales, source, first, columns):
             nc.vector.quantize_mx(
-                out=codes[:, :columns].bitcast(FP8X4),
-                scales=scales[:, :columns],
-                in_=tiles["grouped", n][:, : columns * PACK],
+                out=codes[:, first : first + columns].bitcast(FP8X4),
+                scales=scales[:, first : first + columns],
+                in_=source[:, first * PACK : (first + columns) * PACK],
             )
-            tiles["codes", n] = codes
-            tiles["scales", n] = scales
-            if is_w3(n):
-                g = stream[n][1]
+
+        def quantise_weights(key):
+            w_codes = weights.tile([P, UNIT], U32, align_bytes=64)
+            w_scales = weights.tile([P, UNIT], U8, align_bytes=64)
+            tiles["codes", key] = w_codes
+            tiles["scales", key] = w_scales
+            quantise_columns(w_codes, w_scales, tiles["grouped", key], 0, UNIT)
+            if key != "wo":
                 b3_columns = weights.tile([P, PACK], F32)
-                nc.vector.tensor_copy(out=b3_columns[:], in_=tiles["b3_pairs", g][:])
-                tiles["b3_columns", g] = b3_columns
+                nc.vector.tensor_copy(out=b3_columns[:], in_=tiles["b3_pairs", key[1]][:])
+                tiles["b3_columns", key[1]] = b3_columns
+
+        def weight_key(w):
+            return w if w == "wo" else ("w3", w)
+
+        def weights_regroup(step):
+            for k in (1, 2):
+                w = weight_steps.get(step - k)
+                if w is not None:
+                    regroup_weights(weight_key(w), k - 1, [nc.scalar, nc.vector][k - 1] if w == "wo" else nc.scalar)
+
+        def weights_turn(step):
+            for k in (0, 1):
+                w = weight_steps.get(step - k)
+                if w is not None:
+                    turn(weight_key(w), ROW_TILES, k, "p")
+
+        def weights_quantise(step):
+            w = weight_steps.get(step - 2)
+            if w is not None:
+                quantise_weights(weight_key(w))
+
+        def weights_load(step):
+            w = weight_steps.get(step + 3)
+            if w is not None and w != "wo":
+                load_weights(w, ROW_TILES)
+                load_bo(w)
+
+        def quantise(step, head=False):
+            n, m = step - QUANTISE_H, step - QUANTISE_H3
+            h_columns = P * units[n][2] if is_unit(n) and (head or n >= HEAD_UNITS) else 0
+            h3_columns = P * units[m][2] if is_unit(m) else 0
+            if not h_columns and not h3_columns:
+                return
+            codes = mx_pool.tile([P, 2 * UNIT], U32, align_bytes=64)
+            scales = mx_pool.tile([P, 2 * UNIT], U8, align_bytes=64)
+            if h_columns == UNIT and h3_columns == UNIT:
+                quantise_columns(codes, scales, tiles["values", step], 0, 2 * UNIT)
+            else:
+                if h3_columns:
+                    quantise_columns(codes, scales, tiles["values", step], UNIT, h3_columns)
+                if h_columns:
+                    quantise_columns(codes, scales, tiles["values", step], 0, h_columns)
+            if h_columns:
+                tiles["codes", n] = codes[:, :UNIT]
+                tiles["scales", n] = scales[:, :UNIT]
+            if h3_columns:
+                tiles["h3_codes", m] = codes[:, UNIT:]
+                tiles["h3_scales", m] = scales[:, UNIT:]
 
         def multiply_w3(n, ts):
-            if not is_tokens(n):
+            if not is_unit(n):
                 return
-            w3 = w3_place[stream[n][1]]
-            columns = P * stream[n][3]
+            w3 = ("w3", units[n][0])
+            columns = P * units[n][2]
             for t in ts:
                 hidden = hidden_pool.tile([P, UNIT], F32)
                 nc.tensor.matmul_mx(
@@ -172,10 +232,10 @@ def tile_linearwdecoder_pb_t_kernel(tc, h, W3, b3, Wo, bo, out):
                 tiles["hidden", n, t] = hidden
 
         def bias_relu(n, ts):
-            if not is_tokens(n):
+            if not is_unit(n):
                 return
-            g = stream[n][1]
-            columns = P * stream[n][3]
+            g = units[n][0]
+            columns = P * units[n][2]
             if ts[0] == 0:
                 relu = relu_pool.tile([P, PACK, UNIT], F32)
                 tiles["relu", n] = relu
@@ -211,10 +271,10 @@ def tile_linearwdecoder_pb_t_kernel(tc, h, W3, b3, Wo, bo, out):
             )
 
         def add_residual(n):
-            if not is_tokens(n):
+            if not is_unit(n):
                 return
-            columns = P * (stream[n][3] - (1 if n in shared else 0))
-            h3 = h3_pool.tile([P, UNIT * PACK], BF16, align_bytes=64)
+            columns = P * (units[n][2] - (1 if n in shared else 0))
+            h3 = values_of(n + QUANTISE_H3)[:, UNIT * PACK :]
             nc.vector.tensor_tensor(
                 out=h3[:, : columns * PACK].rearrange("p (c i t) -> p c t i", i=RUN, t=PACK),
                 in0=tiles["relu", n][:, :, :columns].rearrange("p t (c i) -> p c t i", i=RUN),
@@ -223,41 +283,27 @@ def tile_linearwdecoder_pb_t_kernel(tc, h, W3, b3, Wo, bo, out):
             )
             tiles["h3", n] = h3
 
-        def quantise_h3(n):
-            if not is_tokens(n):
-                return
-            columns = P * stream[n][3]
-            h3_codes = h3_pool.tile([P, UNIT], U32, align_bytes=64)
-            h3_scales = h3_pool.tile([P, UNIT], U8, align_bytes=64)
-            nc.vector.quantize_mx(
-                out=h3_codes[:, :columns].bitcast(FP8X4),
-                scales=h3_scales[:, :columns],
-                in_=tiles["h3", n][:, : columns * PACK],
-            )
-            tiles["h3_codes", n] = h3_codes
-            tiles["h3_scales", n] = h3_scales
-
         def multiply_wo(n):
-            if not is_tokens(n):
+            if not is_unit(n):
                 return
-            g = stream[n][1]
+            g = units[n][0]
             projected = projected_pool.tile([P, ROW_TILES, PD], F32)
-            for i in range(stream[n][3]):
+            for i in range(units[n][2]):
                 nc.tensor.matmul_mx(
                     out=projected[:, i, :],
                     lhsT=tiles["h3_codes", n][:, i * P : (i + 1) * P].bitcast(FP8X4),
                     lhsT_scale=tiles["h3_scales", n][:, i * P : (i + 1) * P],
-                    rhs=tiles["codes", wo_place][:, g * PD : (g + 1) * PD].bitcast(FP8X4),
-                    rhs_scale=tiles["scales", wo_place][:, g * PD : (g + 1) * PD],
+                    rhs=tiles["codes", "wo"][:, g * PD : (g + 1) * PD].bitcast(FP8X4),
+                    rhs_scale=tiles["scales", "wo"][:, g * PD : (g + 1) * PD],
                     start=True,
                     stop=True,
                 )
             tiles["projected", n] = projected
 
         def finish(n):
-            if not is_tokens(n):
+            if not is_unit(n):
                 return
-            g, token, size = stream[n][1:4]
+            g, token, size = units[n]
             result = result_pool.tile([P, ROW_TILES, PD], F32)
             nc.vector.tensor_tensor(
                 out=result[:, :size, :],
@@ -270,20 +316,63 @@ def tile_linearwdecoder_pb_t_kernel(tc, h, W3, b3, Wo, bo, out):
 
         first_half, second_half = [0, 1], [2, 3]
         with tc.manual_schedule():
-            for step in range(len(stream) + 9):
+            load_weights(0, PAIR)
+            load(0)
+            load(1)
+            load(2)
+            load_weights("wo", ROW_TILES)
+            load_bo(0)
+            load(3)
+            load(4)
+            for k in range(QUANTISE_H, QUANTISE_H3):
+                values_of(k)
+            turn(("w3", 0), ROW_TILES, 0, "p")
+            turn(("w3", 0), ROW_TILES, 1, "p")
+            regroup_weights(("w3", 0), 0, nc.vector)
+            regroup_weights(("w3", 0), 1, nc.scalar)
+            turn_unit(0, 0)
+            regroup_unit(0, 0, nc.vector)
+            turn_unit(1, 0)
+            regroup_unit(1, 0, nc.vector)
+            quantise_weights(("w3", 0))
+            quantise(QUANTISE_H + 0, True)
+            multiply_w3(0, [0, 1])
+            multiply_w3(0, [2, 3])
+            quantise(QUANTISE_H + 1, True)
+            bias_relu(0, [0, 1])
+            multiply_w3(1, [0, 1])
+            bias_relu(0, [2, 3])
+            multiply_w3(1, [2, 3])
+            bias_relu(1, [0, 1])
+            bias_relu(1, [2, 3])
+            add_residual(0)
+            add_residual(1)
+            for step in range(5, len(units) + 10):
                 load(step)
-                regroup(step - 4, 0)
-                round_sums(step - 8)
-                turn(step - 3, 0)
+                weights_load(step)
+                if step - 7 >= HEAD_UNITS:
+                    add_residual(step - 7)
+                if step - 4 >= HEAD_UNITS:
+                    regroup_unit(step - 4, 0)
+                if step - 3 >= HEAD_UNITS:
+                    turn_unit(step - 3, 0)
+                weights_regroup(step)
+                weights_turn(step)
+                if step - 6 >= HEAD_UNITS:
+                    bias_relu(step - 6, first_half)
+                if step - 4 >= HEAD_UNITS:
+                    regroup_unit(step - 4, 1)
+                weights_quantise(step)
                 multiply_wo(step - 9)
-                bias_relu(step - 6, first_half)
-                multiply_w3(step - 5, first_half)
-                add_on_tensor(step - 7)
-                regroup(step - 4, 1)
-                turn(step - 3, 1)
-                bias_relu(step - 6, second_half)
-                multiply_w3(step - 5, second_half)
-                add_residual(step - 7)
-                quantise_h3(step - 8)
-                quantise(step - 4)
                 finish(step - 9)
+                if step - 6 >= HEAD_UNITS:
+                    bias_relu(step - 6, second_half)
+                add_on_tensor(step - 7)
+                round_sums(step - 7)
+                quantise(step)
+                if step - 5 >= HEAD_UNITS:
+                    multiply_w3(step - 5, first_half)
+                if step - 5 >= HEAD_UNITS:
+                    multiply_w3(step - 5, second_half)
+                if step - 3 >= HEAD_UNITS:
+                    turn_unit(step - 3, 1)

@@ -46,7 +46,7 @@ def tile_linearwdecoder_pb_t_kernel(tc, h, W3, b3, Wo, bo, out):
         values_pool = ctx.enter_context(tc.tile_pool(name="values", bufs=8))
         mx_pool = ctx.enter_context(tc.tile_pool(name="mx", bufs=3))
         relu_pool = ctx.enter_context(tc.tile_pool(name="relu", bufs=4))
-        result_pool = ctx.enter_context(tc.tile_pool(name="result", bufs=3))
+        result_pool = ctx.enter_context(tc.tile_pool(name="result", bufs=6))
         turned_pool = ctx.enter_context(tc.psum_pool(name="turned", bufs=2))
         hidden_pool = ctx.enter_context(tc.psum_pool(name="hidden", bufs=PACK))
         projected_pool = ctx.enter_context(tc.psum_pool(name="projected", bufs=2))
@@ -160,10 +160,6 @@ def tile_linearwdecoder_pb_t_kernel(tc, h, W3, b3, Wo, bo, out):
             tiles["codes", key] = w_codes
             tiles["scales", key] = w_scales
             quantise_columns(w_codes, w_scales, tiles["grouped", key], 0, UNIT)
-            if key != "wo":
-                b3_columns = weights.tile([P, PACK], F32)
-                nc.vector.tensor_copy(out=b3_columns[:], in_=tiles["b3_pairs", key[1]][:])
-                tiles["b3_columns", key[1]] = b3_columns
 
         def weight_key(w):
             return w if w == "wo" else ("w3", w)
@@ -244,7 +240,7 @@ def tile_linearwdecoder_pb_t_kernel(tc, h, W3, b3, Wo, bo, out):
                     out=tiles["relu", n][:, t, :columns],
                     in_=tiles["hidden", n, t][:, :columns],
                     func=RELU,
-                    bias=tiles["b3_columns", g][:, t : t + 1],
+                    bias=tiles["b3_pairs", g][:, t : t + 1],
                 )
 
         def add_on_tensor(n):

@@ -43,10 +43,10 @@ def tile_linearwdecoder_pb_t_kernel(tc, h, W3, b3, Wo, bo, out):
         weights_pool = ctx.enter_context(tc.tile_pool(name="weights_pool", bufs=2))
         weights = ctx.enter_context(tc.tile_pool(name="weights", bufs=G + 1))
         rows_pool = ctx.enter_context(tc.tile_pool(name="rows", bufs=7))
-        values_pool = ctx.enter_context(tc.tile_pool(name="values", bufs=8))
+        values_pool = ctx.enter_context(tc.tile_pool(name="values", bufs=7))
         mx_pool = ctx.enter_context(tc.tile_pool(name="mx", bufs=3))
         relu_pool = ctx.enter_context(tc.tile_pool(name="relu", bufs=4))
-        result_pool = ctx.enter_context(tc.tile_pool(name="result", bufs=6))
+        result_pool = ctx.enter_context(tc.tile_pool(name="result", bufs=len(FIRST_SIZES) + 2 * len(INNER_SIZES) + len(LAST_SIZES)))
         turned_pool = ctx.enter_context(tc.psum_pool(name="turned", bufs=2))
         hidden_pool = ctx.enter_context(tc.psum_pool(name="hidden", bufs=PACK))
         projected_pool = ctx.enter_context(tc.psum_pool(name="projected", bufs=2))

@@ -24,7 +24,8 @@ INNER_SIZES = [ROW_TILES] * 8
 LAST_SIZES = [4, 4, 4, 4, 4, 4, 4, 2, 1, 1]
 
 SHARED_FROM = 1
-SHARED_UNITS = [3, 6]
+SHARED_UNITS = [0, 3, 4, 5, 6, 7]
+SHARED_TOKENS = 64
 
 QUANTISE_H = 4
 QUANTISE_H3 = 8
@@ -246,9 +247,9 @@ def tile_linearwdecoder_pb_t_kernel(tc, h, W3, b3, Wo, bo, out):
         def add_on_tensor(n):
             if n not in shared:
                 return
-            last = slice((ROW_TILES - 1) * P, UNIT)
+            last = slice(UNIT - SHARED_TOKENS, UNIT)
             h_values = tiles["grouped", n][:].rearrange("p (c t) -> p c t", t=PACK)
-            projected = projected_pool.tile([P, ROW_TILES, PD], F32)
+            projected = projected_pool.tile([P, PACK, SHARED_TOKENS], F32)
             for t in range(PACK):
                 nc.tensor.matmul(
                     projected[:, t, :], lhsT=identity[:], rhs=tiles["relu", n][:, t, last], start=True, stop=False
@@ -262,14 +263,14 @@ def tile_linearwdecoder_pb_t_kernel(tc, h, W3, b3, Wo, bo, out):
             if n not in shared:
                 return
             nc.scalar.copy(
-                out=tiles["h3", n][:, (ROW_TILES - 1) * P * PACK :].rearrange("p (c t) -> p c t", t=PACK),
+                out=tiles["h3", n][:, (UNIT - SHARED_TOKENS) * PACK :].rearrange("p (c t) -> p c t", t=PACK),
                 in_=tiles["sums", n][:].rearrange("p t c -> p c t"),
             )
 
         def add_residual(n):
             if not is_unit(n):
                 return
-            columns = P * (units[n][2] - (1 if n in shared else 0))
+            columns = P * units[n][2] - (SHARED_TOKENS if n in shared else 0)
             h3 = values_of(n + QUANTISE_H3)[:, UNIT * PACK :]
             nc.vector.tensor_tensor(
                 out=h3[:, : columns * PACK].rearrange("p (c i t) -> p c t i", i=RUN, t=PACK),

@@ -361,12 +361,12 @@ def tile_linearwdecoder_pb_t_kernel(tc, h, W3, b3, Wo, bo, out):
                     regroup_unit(step - 4, 1)
                 weights_quantise(step)
                 multiply_wo(step - 9)
-                finish(step - 9)
                 if step - 6 >= HEAD_UNITS:
                     bias_relu(step - 6, second_half)
                 add_on_tensor(step - 7)
                 round_sums(step - 7)
                 quantise(step)
+                finish(step - 9)
                 if step - 5 >= HEAD_UNITS:
                     multiply_w3(step - 5, first_half)
                 if step - 5 >= HEAD_UNITS:

from contextlib import ExitStack

import concourse.mybir as mybir
from concourse.masks import make_identity

F32 = mybir.dt.float32
BF16 = mybir.dt.bfloat16
U32 = mybir.dt.uint32
U8 = mybir.dt.uint8
FP8X4 = mybir.dt.float8_e4m3fn_x4
ADD = mybir.AluOpType.add
RELU = mybir.ActivationFunctionType.Relu

B, G, H, PD = 4096, 4, 512, 128
P = 128
PACK = 4
ROW_TILES = 4
UNIT = P * ROW_TILES
PAIR = 2
RUN = 2

FIRST_SIZES = [1, 1, 2, 2, 2, 4, 4, 4, 4, 4, 4]
INNER_SIZES = [ROW_TILES] * 8
LAST_SIZES = [4, 4, 4, 4, 4, 4, 4, 2, 1, 1]

SHARED_FROM = 1
SHARED_UNITS = [0, 3, 4, 5, 6, 7]
SHARED_TOKENS = 64

QUANTISE_H = 4
QUANTISE_H3 = 8
W3_AHEAD = 4
WO_STEP = 5
REGROUP_ON_VECTOR = [(3, 0), (4, 0), (5, 1), (6, 1)]
HEAD_UNITS = 2

FLOPS = 2 * B * G * (H * H + H * PD)


def tile_linearwdecoder_pb_t_kernel(tc, h, W3, b3, Wo, bo, out):
    nc = tc.nc
    with ExitStack() as ctx:
        const = ctx.enter_context(tc.tile_pool(name="const", bufs=1))
        weights_pool = ctx.enter_context(tc.tile_pool(name="weights_pool", bufs=2))
        weights = ctx.enter_context(tc.tile_pool(name="weights", bufs=G + 1))
        rows_pool = ctx.enter_context(tc.tile_pool(name="rows", bufs=7))
        values_pool = ctx.enter_context(tc.tile_pool(name="values", bufs=7))
        mx_pool = ctx.enter_context(tc.tile_pool(name="mx", bufs=3))
        relu_pool = ctx.enter_context(tc.tile_pool(name="relu", bufs=4))
        result_pool = ctx.enter_context(tc.tile_pool(name="result", bufs=len(FIRST_SIZES) + 2 * len(INNER_SIZES) + len(LAST_SIZES)))
        turned_pool = ctx.enter_context(tc.psum_pool(name="turned", bufs=2))
        hidden_pool = ctx.enter_context(tc.psum_pool(name="hidden", bufs=PACK))
        projected_pool = ctx.enter_context(tc.psum_pool(name="projected", bufs=2))

        identity = const.tile([P, P], F32)
        make_identity(nc, identity[:])
        identity_bf16 = const.tile([P, P], BF16)
        make_identity(nc, identity_bf16[:])

        units = []
        first_of = []
        for g in range(G):
            first_of.append(len(units))
            sizes = FIRST_SIZES if g == 0 else LAST_SIZES if g == G - 1 else INNER_SIZES
            token = 0
            for size in sizes:
                units.append((g, token, size))
                token += P * size
        shared = [n for n, (g, token, size) in enumerate(units) if size == ROW_TILES and g >= SHARED_FROM and token // UNIT in SHARED_UNITS]
        weight_steps = {WO_STEP: "wo"}
        for g in range(1, G):
            weight_steps[first_of[g] + QUANTISE_H - W3_AHEAD] = g
        tiles = {}

        def is_unit(n):
            return 0 <= n < len(units)

        def load_rows(key, view, size, step):
            rows = rows_pool.tile([P, ROW_TILES, H], BF16)
            for i in range(0, size, step):
                nc.sync.dma_start(out=rows[:, i : i + step, :], in_=view[:, i : i + step, :])
            tiles["rows", key] = rows

        def load_weights(w, step):
            if w == "wo":
                load_rows(w, Wo.rearrange("g p k -> p g k"), ROW_TILES, step)
                return
            load_rows(("w3", w), W3[w].rearrange("(p t) k -> p t k", t=PACK), ROW_TILES, step)
            b3_pairs = weights.tile([P, PACK], BF16)
            nc.scalar.dma_start(out=b3_pairs[:], in_=b3[w].rearrange("(p t) -> p t", t=PACK))
            tiles["b3_pairs", w] = b3_pairs

        def load_bo(g):
            bo_rows = weights.tile([P, PD], BF16)
            nc.sync.dma_start(out=bo_rows[:], in_=bo[g].partition_broadcast(P))
            tiles["bo_rows", g] = bo_rows

        def load(n):
            if is_unit(n):
                g, token, size = units[n]
                load_rows(n, h[token : token + P * size, g, :].rearrange("(p i) k -> p i k", i=size), size, size)

        def turn(key, size, pair, bank=None):
            if pair * PAIR >= size:
                return
            if bank is None:
                turned = turned_pool.tile([P, 2, PAIR * P], F32)
            else:
                turned = projected_pool.tile([P, 2, PAIR * P], F32, tag="projected", name="projected")
            tiles["turned", key, pair] = turned
            for i in range(pair * PAIR, min((pair + 1) * PAIR, size)):
                words = tiles["rows", key][:, i, :].bitcast(F32)
                j = i % PAIR
                for u in range(2):
                    nc.tensor.transpose(turned[:, u, j * P : (j + 1) * P], words[:, u : 2 * P : 2], identity[:])

        def turn_unit(n, pair):
            if is_unit(n):
                turn(n, units[n][2], pair)

        def values_of(step):
            if ("values", step) not in tiles:
                values = values_pool.tile([P, 2 * UNIT * PACK], BF16, align_bytes=64)
                tiles["values", step] = values
            return tiles["values", step]

        def regroup(key, size, pair, engine):
            if pair * PAIR >= size:
                return
            grouped_words = tiles["grouped", key].bitcast(F32).rearrange("p (c u) -> p c u", u=2)
            columns = slice(pair * PAIR * P, min((pair + 1) * PAIR, size) * P)
            width = columns.stop - columns.start
            copy = engine.copy if engine is nc.scalar else engine.tensor_copy
            copy(
                out=grouped_words[:, columns, :],
                in_=tiles["turned", key, pair][:, :, :width].rearrange("p u c -> p c u"),
            )

        def regroup_unit(n, pair, engine=nc.scalar):
            if is_unit(n):
                if pair == 0:
                    tiles["grouped", n] = values_of(n + QUANTISE_H)[:, : UNIT * PACK]
                regroup(n, units[n][2], pair, nc.vector if (n, pair) in REGROUP_ON_VECTOR else engine)

        def regroup_weights(key, pair, engine):
            if pair == 0:
                w_grouped = weights_pool.tile([P, UNIT * PACK], BF16, align_bytes=64)
                tiles["grouped", key] = w_grouped[:]
            regroup(key, ROW_TILES, pair, engine)

        def quantise_columns(codes, scales, source, first, columns):
            nc.vector.quantize_mx(
                out=codes[:, first : first + columns].bitcast(FP8X4),
                scales=scales[:, first : first + columns],
                in_=source[:, first * PACK : (first + columns) * PACK],
            )

        def quantise_weights(key):
            w_codes = weights.tile([P, UNIT], U32, align_bytes=64)
            w_scales = weights.tile([P, UNIT], U8, align_bytes=64)
            tiles["codes", key] = w_codes
            tiles["scales", key] = w_scales
            quantise_columns(w_codes, w_scales, tiles["grouped", key], 0, UNIT)

        def weight_key(w):
            return w if w == "wo" else ("w3", w)

        def weights_regroup(step):
            for k in (1, 2):
                w = weight_steps.get(step - k)
                if w is not None:
                    regroup_weights(weight_key(w), k - 1, [nc.scalar, nc.vector][k - 1] if w == "wo" else nc.scalar)

        def weights_turn(step):
            for k in (0, 1):
                w = weight_steps.get(step - k)
                if w is not None:
                    turn(weight_key(w), ROW_TILES, k, "p")

        def weights_quantise(step):
            w = weight_steps.get(step - 2)
            if w is not None:
                quantise_weights(weight_key(w))

        def weights_load(step):
            w = weight_steps.get(step + 3)
            if w is not None and w != "wo":
                load_weights(w, ROW_TILES)
                load_bo(w)

        def quantise(step, head=False):
            n, m = step - QUANTISE_H, step - QUANTISE_H3
            h_columns = P * units[n][2] if is_unit(n) and (head or n >= HEAD_UNITS) else 0
            h3_columns = P * units[m][2] if is_unit(m) else 0
            if not h_columns and not h3_columns:
                return
            codes = mx_pool.tile([P, 2 * UNIT], U32, align_bytes=64)
            scales = mx_pool.tile([P, 2 * UNIT], U8, align_bytes=64)
            if h_columns == UNIT and h3_columns == UNIT:
                quantise_columns(codes, scales, tiles["values", step], 0, 2 * UNIT)
            else:
                if h3_columns:
                    quantise_columns(codes, scales, tiles["values", step], UNIT, h3_columns)
                if h_columns:
                    quantise_columns(codes, scales, tiles["values", step], 0, h_columns)
            if h_columns:
                tiles["codes", n] = codes[:, :UNIT]
                tiles["scales", n] = scales[:, :UNIT]
            if h3_columns:
                tiles["h3_codes", m] = codes[:, UNIT:]
                tiles["h3_scales", m] = scales[:, UNIT:]

        def multiply_w3(n, ts):
            if not is_unit(n):
                return
            w3 = ("w3", units[n][0])
            columns = P * units[n][2]
            for t in ts:
                hidden = hidden_pool.tile([P, UNIT], F32)
                nc.tensor.matmul_mx(
                    out=hidden[:, :columns],
                    lhsT=tiles["codes", w3][:, t * P : (t + 1) * P].bitcast(FP8X4),
                    lhsT_scale=tiles["scales", w3][:, t * P : (t + 1) * P],
                    rhs=tiles["codes", n][:, :columns].bitcast(FP8X4),
                    rhs_scale=tiles["scales", n][:, :columns],
                    start=True,
                    stop=True,
                )
                tiles["hidden", n, t] = hidden

        def bias_relu(n, ts):
            if not is_unit(n):
                return
            g = units[n][0]
            columns = P * units[n][2]
            if ts[0] == 0:
                relu = relu_pool.tile([P, PACK, UNIT], F32)
                tiles["relu", n] = relu
            for t in ts:
                nc.scalar.activation(
                    out=tiles["relu", n][:, t, :columns],
                    in_=tiles["hidden", n, t][:, :columns],
                    func=RELU,
                    bias=tiles["b3_pairs", g][:, t : t + 1],
                )

        def add_on_tensor(n):
            if n not in shared:
                return
            last = slice(UNIT - SHARED_TOKENS, UNIT)
            h_values = tiles["grouped", n][:].rearrange("p (c t) -> p c t", t=PACK)
            projected = projected_pool.tile([P, PACK, SHARED_TOKENS], F32)
            for t in range(PACK):
                nc.tensor.matmul(
                    projected[:, t, :], lhsT=identity[:], rhs=tiles["relu", n][:, t, last], start=True, stop=False
                )
                nc.tensor.matmul(
                    projected[:, t, :], lhsT=identity_bf16[:], rhs=h_values[:, last, t], start=False, stop=True
                )
            tiles["sums", n] = projected

        def round_sums(n):
            if n not in shared:
                return
            nc.scalar.copy(
                out=tiles["h3", n][:, (UNIT - SHARED_TOKENS) * PACK :].rearrange("p (c t) -> p c t", t=PACK),
                in_=tiles["sums", n][:].rearrange("p t c -> p c t"),
            )

        def add_residual(n):
            if not is_unit(n):
                return
            columns = P * units[n][2] - (SHARED_TOKENS if n in shared else 0)
            h3 = values_of(n + QUANTISE_H3)[:, UNIT * PACK :]
            nc.vector.tensor_tensor(
                out=h3[:, : columns * PACK].rearrange("p (c i t) -> p c t i", i=RUN, t=PACK),
                in0=tiles["relu", n][:, :, :columns].rearrange("p t (c i) -> p c t i", i=RUN),
                in1=tiles["grouped", n][:, : columns * PACK].rearrange("p (c i t) -> p c t i", i=RUN, t=PACK),
                op=ADD,
            )
            tiles["h3", n] = h3

        def multiply_wo(n):
            if not is_unit(n):
                return
            g = units[n][0]
            projected = projected_pool.tile([P, ROW_TILES, PD], F32)
            for i in range(units[n][2]):
                nc.tensor.matmul_mx(
                    out=projected[:, i, :],
                    lhsT=tiles["h3_codes", n][:, i * P : (i + 1) * P].bitcast(FP8X4),
                    lhsT_scale=tiles["h3_scales", n][:, i * P : (i + 1) * P],
                    rhs=tiles["codes", "wo"][:, g * PD : (g + 1) * PD].bitcast(FP8X4),
                    rhs_scale=tiles["scales", "wo"][:, g * PD : (g + 1) * PD],
                    start=True,
                    stop=True,
                )
            tiles["projected", n] = projected

        def finish(n):
            if not is_unit(n):
                return
            g, token, size = units[n]
            result = result_pool.tile([P, ROW_TILES, PD], F32)
            nc.vector.tensor_tensor(
                out=result[:, :size, :],
                in0=tiles["projected", n][:, :size, :],
                in1=tiles["bo_rows", g][:].unsqueeze(1).to_broadcast([P, size, PD]),
                op=ADD,
            )
            rows = out[token : token + P * size, g * PD : (g + 1) * PD]
            nc.sync.dma_start(out=rows.rearrange("(p i) n -> p i n", i=size), in_=result[:, :size, :])

        first_half, second_half = [0, 1], [2, 3]
        with tc.manual_schedule():
            load_weights(0, PAIR)
            load(0)
            load(1)
            load(2)
            load_weights("wo", ROW_TILES)
            load_bo(0)
            load(3)
            load(4)
            for k in range(QUANTISE_H, QUANTISE_H3):
                values_of(k)
            turn(("w3", 0), ROW_TILES, 0, "p")
            turn(("w3", 0), ROW_TILES, 1, "p")
            regroup_weights(("w3", 0), 0, nc.vector)
            regroup_weights(("w3", 0), 1, nc.scalar)
            turn_unit(0, 0)
            regroup_unit(0, 0, nc.vector)
            turn_unit(1, 0)
            regroup_unit(1, 0, nc.vector)
            quantise_weights(("w3", 0))
            quantise(QUANTISE_H + 0, True)
            multiply_w3(0, [0, 1])
            multiply_w3(0, [2, 3])
            quantise(QUANTISE_H + 1, True)
            bias_relu(0, [0, 1])
            multiply_w3(1, [0, 1])
            bias_relu(0, [2, 3])
            multiply_w3(1, [2, 3])
            bias_relu(1, [0, 1])
            bias_relu(1, [2, 3])
            add_residual(0)
            add_residual(1)
            for step in range(5, len(units) + 10):
                load(step)
                weights_load(step)
                if step - 7 >= HEAD_UNITS:
                    add_residual(step - 7)
                if step - 4 >= HEAD_UNITS:
                    regroup_unit(step - 4, 0)
                if step - 3 >= HEAD_UNITS:
                    turn_unit(step - 3, 0)
                weights_regroup(step)
                weights_turn(step)
                if step - 6 >= HEAD_UNITS:
                    bias_relu(step - 6, first_half)
                if step - 4 >= HEAD_UNITS:
                    regroup_unit(step - 4, 1)
                weights_quantise(step)
                multiply_wo(step - 9)
                if step - 6 >= HEAD_UNITS:
                    bias_relu(step - 6, second_half)
                add_on_tensor(step - 7)
                round_sums(step - 7)
                quantise(step)
                finish(step - 9)
                if step - 5 >= HEAD_UNITS:
                    multiply_w3(step - 5, first_half)
                if step - 5 >= HEAD_UNITS:
                    multiply_w3(step - 5, second_half)
                if step - 3 >= HEAD_UNITS:
                    turn_unit(step - 3, 1)
